import numpy as np
import ml_dtypes

BF16 = ml_dtypes.bfloat16


def bf(x):
    return np.asarray(x, np.float32).astype(BF16)


def f32(x):
    return np.asarray(x, np.float32)


def f64(x):
    return np.asarray(x).astype(np.float64)


def striped(idx):
    return np.tile(idx.reshape(-1, 16).T, (8, 1))


C, E, S, N, Q = 256, 256, 512, 128, 4


def sigmoid(a):
    return 1.0 / (1.0 + np.exp(-a))


def setup_inputs():
    return {
        "base": f32(0.5 * np.random.standard_normal((C, S))),
        "emb": bf(np.random.standard_normal((E, N))),
        "h_prev": bf(np.random.standard_normal((C, N))),
        "c_prev": f32(np.random.standard_normal((C, N))),
        "w_ih": bf(np.random.standard_normal((E, Q * C)) / np.sqrt(E)),
        "w_hh": bf(np.random.standard_normal((C, Q * C)) / np.sqrt(C)),
        "b": f32(0.5 * np.random.standard_normal((Q * C, 1))),
        "offs": striped(np.random.permutation(S)[:N]),
    }


def reference(base, emb, h_prev, c_prev, w_ih, w_hh, b, offs):
    idx = offs[:16].T.reshape(-1)
    z = f64(w_ih).T @ np.maximum(f64(emb), 0.0) + f64(w_hh).T @ f64(h_prev) + f64(b)
    zi, zf, zu, zo = np.split(z, Q, axis=0)
    c_new = sigmoid(zf) * f64(c_prev) + sigmoid(zi) * np.tanh(zu)
    res = f64(base).copy()
    res[:, idx] = sigmoid(zo) * np.tanh(c_new)
    return res

@@ -1,0 +1,78 @@
+import concourse.mybir as mybir
+from concourse.masks import make_identity
+
+P = 128
+C, E, S, N, Q = 256, 256, 512, 128, 4
+CB = C // P
+KB = E // P
+GATE_I, GATE_F, GATE_U, GATE_O = 0, 1, 2, 3
+
+FLOPS = 2 * (E + C) * Q * C * N
+
+BF16, F32, U16 = mybir.dt.bfloat16, mybir.dt.float32, mybir.dt.uint16
+MULT, ADD = mybir.AluOpType.mult, mybir.AluOpType.add
+SIGMOID, TANH = mybir.ActivationFunctionType.Sigmoid, mybir.ActivationFunctionType.Tanh
+
+
+def tile_capatt_kernel(tc, base, emb, h_prev, c_prev, w_ih, w_hh, b, offs, out):
+    nc = tc.nc
+    with (
+        tc.tile_pool(name="held", bufs=1) as held,
+        tc.tile_pool(name="work", bufs=2) as work,
+        tc.psum_pool(name="psum_bias", bufs=1) as psum_bias,
+        tc.psum_pool(name="psum_z", bufs=4) as psum_z,
+    ):
+        offsets = held.tile([P, N // 16], U16, name="offsets")
+        nc.sync.dma_start(offsets[:], offs)
+
+        emb_sb = held.tile([P, KB, N], BF16, name="emb_sb")
+        h_sb = held.tile([P, KB, N], BF16, name="h_sb")
+        w_ih_sb = held.tile([P, KB, Q * C], BF16, name="w_ih_sb")
+        w_hh_sb = held.tile([P, KB, Q * C], BF16, name="w_hh_sb")
+        c_sb = held.tile([P, CB, N], F32, name="c_sb")
+        b_rows = held.tile([Q * CB, P], F32, name="b_rows")
+        windows = [held.tile([P, S], F32, name=f"window{cb}") for cb in range(CB)]
+
+        nc.sync.dma_start(emb_sb[:], emb.rearrange("(k p) n -> p k n", p=P))
+        nc.scalar.dma_start(h_sb[:], h_prev.rearrange("(k p) n -> p k n", p=P))
+        nc.scalar.dma_start(b_rows[:], b.rearrange("(g p) o -> g (p o)", p=P))
+        nc.sync.dma_start(w_ih_sb[:], w_ih.rearrange("(k p) r -> p k r", p=P))
+        nc.scalar.dma_start(w_hh_sb[:], w_hh.rearrange("(k p) r -> p k r", p=P))
+        nc.sync.dma_start(c_sb[:], c_prev.rearrange("(k p) n -> p k n", p=P))
+        nc.sync.dma_start(windows[0][:], base[0:P, :])
+        nc.scalar.dma_start(windows[1][:], base[P : 2 * P, :])
+
+        identity = held.tile([Q * CB, Q * CB], F32, name="identity")
+        make_identity(nc, identity[:])
+        bias_ps = psum_bias.tile([P, Q * CB], F32, name="bias_ps")
+        nc.tensor.matmul(bias_ps[:], b_rows[:], identity[:], start=True, stop=True)
+        bias_sb = held.tile([P, Q * CB], F32, name="bias_sb")
+        nc.vector.tensor_copy(bias_sb[:], bias_ps[:])
+
+        relu_sb = held.tile([P, KB, N], BF16, name="relu_sb")
+        nc.vector.tensor_scalar_max(relu_sb[:], emb_sb[:], 0.0)
+
+        for cb in range(CB):
+            gate = {}
+            for q, func in ((GATE_F, SIGMOID), (GATE_I, SIGMOID), (GATE_U, TANH), (GATE_O, SIGMOID)):
+                g = q * CB + cb
+                rows = slice(g * P, (g + 1) * P)
+                z = psum_z.tile([P, N], F32, name="z")
+                for k in range(KB):
+                    nc.tensor.matmul(z[:], w_hh_sb[:, k, rows], h_sb[:, k, :], start=(k == 0), stop=False)
+                for k in range(KB):
+                    nc.tensor.matmul(z[:], w_ih_sb[:, k, rows], relu_sb[:, k, :], start=False, stop=(k == KB - 1))
+                gate[q] = work.tile([P, N], F32, name=f"gate{q}")
+                nc.scalar.activation(gate[q][:], z[:], func, bias=bias_sb[:, g : g + 1])
+
+            kept = work.tile([P, N], F32, name="kept")
+            nc.vector.tensor_tensor(kept[:], gate[GATE_F][:], c_sb[:, cb, :], MULT)
+            fresh = work.tile([P, N], F32, name="fresh")
+            nc.vector.tensor_tensor(fresh[:], gate[GATE_I][:], gate[GATE_U][:], MULT)
+            c_new = work.tile([P, N], F32, name="c_new")
+            nc.vector.tensor_tensor(c_new[:], kept[:], fresh[:], ADD)
+            tanh_c = work.tile([P, N], F32, name="tanh_c")
+            nc.scalar.activation(tanh_c[:], c_new[:], TANH)
+
+            nc.vector.tensor_tensor(windows[cb][:].indirect(offsets[:]), gate[GATE_O][:], tanh_c[:], MULT)
+            nc.sync.dma_start(out[cb * P : (cb + 1) * P, :], windows[cb][:])

@@ -6,6 +6,7 @@ C, E, S, N, Q = 256, 256, 512, 128, 4
 CB = C // P
 KB = E // P
 GATE_I, GATE_F, GATE_U, GATE_O = 0, 1, 2, 3
+WARM_MATMULS = 20
 
 FLOPS = 2 * (E + C) * Q * C * N
 
@@ -18,61 +19,99 @@ def tile_capatt_kernel(tc, base, emb, h_prev, c_prev, w_ih, w_hh, b, offs, out):
     nc = tc.nc
     with (
         tc.tile_pool(name="held", bufs=1) as held,
-        tc.tile_pool(name="work", bufs=2) as work,
+        tc.psum_pool(name="psum_warm", bufs=1) as psum_warm,
         tc.psum_pool(name="psum_bias", bufs=1) as psum_bias,
-        tc.psum_pool(name="psum_z", bufs=4) as psum_z,
+        tc.psum_pool(name="psum_z", bufs=6) as psum_z,
     ):
+        warm_sb = held.tile([P, P], BF16, name="warm_sb")
+        nc.vector.memset(warm_sb[:], 0.0)
+        warm_ps = psum_warm.tile([P, P], F32, name="warm_ps")
+        for i in range(WARM_MATMULS):
+            nc.tensor.matmul(warm_ps[:], warm_sb[:], warm_sb[:], start=True, stop=True)
+
+        h_sb = held.tile([P, KB, N], BF16, name="h_sb")
+        nc.sync.dma_start(h_sb[:], h_prev.rearrange("(k p) n -> p k n", p=P))
+        emb_sb = held.tile([P, KB, N], BF16, name="emb_sb")
+        nc.scalar.dma_start(emb_sb[:], emb.rearrange("(k p) n -> p k n", p=P))
+        b_rows = held.tile([Q * CB, P], F32, name="b_rows")
+        nc.scalar.dma_start(b_rows[:], b.rearrange("(g p) o -> g (p o)", p=P))
+
+        w_sb = {}
+        for piece, (first_gate, gates) in enumerate(((GATE_I, 2), (GATE_U, 1), (GATE_O, 1))):
+            for name, w in (("hh", w_hh), ("ih", w_ih)):
+                w_piece = held.tile([P, KB, gates * C], BF16, name=f"w_{name}{piece}")
+                cols = w[:, first_gate * C : (first_gate + gates) * C]
+                nc.sync.dma_start(w_piece[:], cols.rearrange("(k p) r -> p k r", p=P))
+                for q in range(first_gate, first_gate + gates):
+                    w_sb[name, q] = w_piece[:, :, (q - first_gate) * C : (q - first_gate + 1) * C]
+
+        c_sb = held.tile([P, CB, N], F32, name="c_sb")
+        nc.sync.dma_start(c_sb[:], c_prev.rearrange("(k p) n -> p k n", p=P))
         offsets = held.tile([P, N // 16], U16, name="offsets")
         nc.sync.dma_start(offsets[:], offs)
-
-        emb_sb = held.tile([P, KB, N], BF16, name="emb_sb")
-        h_sb = held.tile([P, KB, N], BF16, name="h_sb")
-        w_ih_sb = held.tile([P, KB, Q * C], BF16, name="w_ih_sb")
-        w_hh_sb = held.tile([P, KB, Q * C], BF16, name="w_hh_sb")
-        c_sb = held.tile([P, CB, N], F32, name="c_sb")
-        b_rows = held.tile([Q * CB, P], F32, name="b_rows")
         windows = [held.tile([P, S], F32, name=f"window{cb}") for cb in range(CB)]
-
-        nc.sync.dma_start(emb_sb[:], emb.rearrange("(k p) n -> p k n", p=P))
-        nc.scalar.dma_start(h_sb[:], h_prev.rearrange("(k p) n -> p k n", p=P))
-        nc.scalar.dma_start(b_rows[:], b.rearrange("(g p) o -> g (p o)", p=P))
-        nc.sync.dma_start(w_ih_sb[:], w_ih.rearrange("(k p) r -> p k r", p=P))
-        nc.scalar.dma_start(w_hh_sb[:], w_hh.rearrange("(k p) r -> p k r", p=P))
-        nc.sync.dma_start(c_sb[:], c_prev.rearrange("(k p) n -> p k n", p=P))
-        nc.sync.dma_start(windows[0][:], base[0:P, :])
-        nc.scalar.dma_start(windows[1][:], base[P : 2 * P, :])
+        for cb in range(CB):
+            nc.sync.dma_start(windows[cb][:], base[cb * P : (cb + 1) * P, :])
 
         identity = held.tile([Q * CB, Q * CB], F32, name="identity")
         make_identity(nc, identity[:])
+
+        relu_sb = held.tile([P, KB, N], BF16, name="relu_sb")
+        nc.vector.tensor_scalar_max(relu_sb[:], emb_sb[:], 0.0)
+
+        x_of = {"hh": h_sb, "ih": relu_sb}
+        func_of = {GATE_I: SIGMOID, GATE_F: SIGMOID, GATE_U: TANH, GATE_O: SIGMOID}
+        z = {}
+        gate = {}
+
+        def add_part(q, cb, name):
+            if name == "hh":
+                z[q, cb] = psum_z.tile([P, N], F32, name="z")
+            for k in range(KB):
+                nc.tensor.matmul(
+                    z[q, cb][:],
+                    w_sb[name, q][:, k, cb * P : (cb + 1) * P],
+                    x_of[name][:, k, :],
+                    start=(name == "hh" and k == 0),
+                    stop=(name == "ih" and k == KB - 1),
+                )
+
+        def activate(q, cb):
+            g = q * CB + cb
+            gate[q, cb] = held.tile([P, N], F32, name=f"gate{q}_{cb}")
+            nc.scalar.activation(gate[q, cb][:], z[q, cb][:], func_of[q], bias=bias_sb[:, g : g + 1])
+
+        for cb in range(CB):
+            for q in (GATE_I, GATE_F):
+                add_part(q, cb, "hh")
+
         bias_ps = psum_bias.tile([P, Q * CB], F32, name="bias_ps")
         nc.tensor.matmul(bias_ps[:], b_rows[:], identity[:], start=True, stop=True)
         bias_sb = held.tile([P, Q * CB], F32, name="bias_sb")
         nc.vector.tensor_copy(bias_sb[:], bias_ps[:])
 
-        relu_sb = held.tile([P, KB, N], BF16, name="relu_sb")
-        nc.vector.tensor_scalar_max(relu_sb[:], emb_sb[:], 0.0)
+        c_new = {}
+        for cb in range(CB):
+            for q in (GATE_I, GATE_F):
+                add_part(q, cb, "ih")
+                activate(q, cb)
+            add_part(GATE_U, cb, "hh")
+            add_part(GATE_U, cb, "ih")
+            activate(GATE_U, cb)
+            kept = held.tile([P, N], F32, name=f"kept{cb}")
+            nc.vector.tensor_tensor(kept[:], gate[GATE_F, cb][:], c_sb[:, cb, :], MULT)
+            fresh = held.tile([P, N], F32, name=f"fresh{cb}")
+            nc.vector.tensor_tensor(fresh[:], gate[GATE_I, cb][:], gate[GATE_U, cb][:], MULT)
+            c_new[cb] = held.tile([P, N], F32, name=f"c_new{cb}")
+            nc.vector.tensor_tensor(c_new[cb][:], kept[:], fresh[:], ADD)
 
         for cb in range(CB):
-            gate = {}
-            for q, func in ((GATE_F, SIGMOID), (GATE_I, SIGMOID), (GATE_U, TANH), (GATE_O, SIGMOID)):
-                g = q * CB + cb
-                rows = slice(g * P, (g + 1) * P)
-                z = psum_z.tile([P, N], F32, name="z")
-                for k in range(KB):
-                    nc.tensor.matmul(z[:], w_hh_sb[:, k, rows], h_sb[:, k, :], start=(k == 0), stop=False)
-                for k in range(KB):
-                    nc.tensor.matmul(z[:], w_ih_sb[:, k, rows], relu_sb[:, k, :], start=False, stop=(k == KB - 1))
-                gate[q] = work.tile([P, N], F32, name=f"gate{q}")
-                nc.scalar.activation(gate[q][:], z[:], func, bias=bias_sb[:, g : g + 1])
+            add_part(GATE_O, cb, "hh")
+            add_part(GATE_O, cb, "ih")
+            activate(GATE_O, cb)
 
-            kept = work.tile([P, N], F32, name="kept")
-            nc.vector.tensor_tensor(kept[:], gate[GATE_F][:], c_sb[:, cb, :], MULT)
-            fresh = work.tile([P, N], F32, name="fresh")
-            nc.vector.tensor_tensor(fresh[:], gate[GATE_I][:], gate[GATE_U][:], MULT)
-            c_new = work.tile([P, N], F32, name="c_new")
-            nc.vector.tensor_tensor(c_new[:], kept[:], fresh[:], ADD)
-            tanh_c = work.tile([P, N], F32, name="tanh_c")
-            nc.scalar.activation(tanh_c[:], c_new[:], TANH)
-
-            nc.vector.tensor_tensor(windows[cb][:].indirect(offsets[:]), gate[GATE_O][:], tanh_c[:], MULT)
+        for cb in range(CB):
+            tanh_c = held.tile([P, N], F32, name=f"tanh_c{cb}")
+            nc.scalar.activation(tanh_c[:], c_new[cb][:], TANH)
+            nc.vector.tensor_tensor(windows[cb][:].indirect(offsets[:]), gate[GATE_O, cb][:], tanh_c[:], MULT)
             nc.sync.dma_start(out[cb * P : (cb + 1) * P, :], windows[cb][:])

@@ -6,7 +6,6 @@ C, E, S, N, Q = 256, 256, 512, 128, 4
 CB = C // P
 KB = E // P
 GATE_I, GATE_F, GATE_U, GATE_O = 0, 1, 2, 3
-WARM_MATMULS = 20
 
 FLOPS = 2 * (E + C) * Q * C * N
 
@@ -19,16 +18,9 @@ def tile_capatt_kernel(tc, base, emb, h_prev, c_prev, w_ih, w_hh, b, offs, out):
     nc = tc.nc
     with (
         tc.tile_pool(name="held", bufs=1) as held,
-        tc.psum_pool(name="psum_warm", bufs=1) as psum_warm,
         tc.psum_pool(name="psum_bias", bufs=1) as psum_bias,
         tc.psum_pool(name="psum_z", bufs=6) as psum_z,
     ):
-        warm_sb = held.tile([P, P], BF16, name="warm_sb")
-        nc.vector.memset(warm_sb[:], 0.0)
-        warm_ps = psum_warm.tile([P, P], F32, name="warm_ps")
-        for i in range(WARM_MATMULS):
-            nc.tensor.matmul(warm_ps[:], warm_sb[:], warm_sb[:], start=True, stop=True)
-
         h_sb = held.tile([P, KB, N], BF16, name="h_sb")
         nc.sync.dma_start(h_sb[:], h_prev.rearrange("(k p) n -> p k n", p=P))
         emb_sb = held.tile([P, KB, N], BF16, name="emb_sb")

@@ -1,11 +1,12 @@
 import concourse.mybir as mybir
-from concourse.masks import make_identity
 
 P = 128
+T = 32
 C, E, S, N, Q = 256, 256, 512, 128, 4
 CB = C // P
 KB = E // P
 GATE_I, GATE_F, GATE_U, GATE_O = 0, 1, 2, 3
+WARM_MATMULS = 20
 
 FLOPS = 2 * (E + C) * Q * C * N
 
@@ -18,15 +19,25 @@ def tile_capatt_kernel(tc, base, emb, h_prev, c_prev, w_ih, w_hh, b, offs, out):
     nc = tc.nc
     with (
         tc.tile_pool(name="held", bufs=1) as held,
-        tc.psum_pool(name="psum_bias", bufs=1) as psum_bias,
-        tc.psum_pool(name="psum_z", bufs=6) as psum_z,
+        tc.psum_pool(name="psum_warm", bufs=1) as psum_warm,
+        tc.psum_pool(name="psum_z", bufs=7) as psum_z,
     ):
+        warm_sb = held.tile([P, P], BF16, name="warm_sb")
+        nc.vector.memset(warm_sb[:], 0.0)
+        warm_ps = psum_warm.tile([P, P], F32, name="warm_ps")
+        for i in range(WARM_MATMULS):
+            nc.tensor.matmul(warm_ps[:], warm_sb[:], warm_sb[:], start=True, stop=True)
+
         h_sb = held.tile([P, KB, N], BF16, name="h_sb")
         nc.sync.dma_start(h_sb[:], h_prev.rearrange("(k p) n -> p k n", p=P))
         emb_sb = held.tile([P, KB, N], BF16, name="emb_sb")
         nc.scalar.dma_start(emb_sb[:], emb.rearrange("(k p) n -> p k n", p=P))
-        b_rows = held.tile([Q * CB, P], F32, name="b_rows")
-        nc.scalar.dma_start(b_rows[:], b.rearrange("(g p) o -> g (p o)", p=P))
+
+        b_blocks = held.tile([P, T], F32, name="b_blocks", align_bytes=64)
+        nc.gpsimd.memset(b_blocks[:], 0.0)
+        b_runs = b.rearrange("(g a c) o -> a g (c o)", a=P // T, c=T)
+        for a in range(P // T):
+            nc.scalar.dma_start(b_blocks[a * T : a * T + Q * CB, :], b_runs[a])
 
         w_sb = {}
         for piece, (first_gate, gates) in enumerate(((GATE_I, 2), (GATE_U, 1), (GATE_O, 1))):
@@ -45,11 +56,11 @@ def tile_capatt_kernel(tc, base, emb, h_prev, c_prev, w_ih, w_hh, b, offs, out):
         for cb in range(CB):
             nc.sync.dma_start(windows[cb][:], base[cb * P : (cb + 1) * P, :])
 
-        identity = held.tile([Q * CB, Q * CB], F32, name="identity")
-        make_identity(nc, identity[:])
-
         relu_sb = held.tile([P, KB, N], BF16, name="relu_sb")
         nc.vector.tensor_scalar_max(relu_sb[:], emb_sb[:], 0.0)
+
+        bias_sb = held.tile([P, T], F32, name="bias_sb", align_bytes=64)
+        nc.vector.transpose(bias_sb[:], b_blocks[:])
 
         x_of = {"hh": h_sb, "ih": relu_sb}
         func_of = {GATE_I: SIGMOID, GATE_F: SIGMOID, GATE_U: TANH, GATE_O: SIGMOID}
@@ -76,11 +87,6 @@ def tile_capatt_kernel(tc, base, emb, h_prev, c_prev, w_ih, w_hh, b, offs, out):
         for cb in range(CB):
             for q in (GATE_I, GATE_F):
                 add_part(q, cb, "hh")
-
-        bias_ps = psum_bias.tile([P, Q * CB], F32, name="bias_ps")
-        nc.tensor.matmul(bias_ps[:], b_rows[:], identity[:], start=True, stop=True)
-        bias_sb = held.tile([P, Q * CB], F32, name="bias_sb")
-        nc.vector.tensor_copy(bias_sb[:], bias_ps[:])
 
         c_new = {}
         for cb in range(CB):

@@ -1,7 +1,6 @@
 import concourse.mybir as mybir
 
 P = 128
-T = 32
 C, E, S, N, Q = 256, 256, 512, 128, 4
 CB = C // P
 KB = E // P
@@ -28,16 +27,13 @@ def tile_capatt_kernel(tc, base, emb, h_prev, c_prev, w_ih, w_hh, b, offs, out):
         for i in range(WARM_MATMULS):
             nc.tensor.matmul(warm_ps[:], warm_sb[:], warm_sb[:], start=True, stop=True)
 
+        bias_sb = held.tile([P, Q * CB], F32, name="bias_sb")
+        with nc.allow_non_contiguous_dma(reason="b is turned from rows into columns by the load"):
+            nc.scalar.dma_start(bias_sb[:], b.rearrange("(g p) o -> p (g o)", p=P))
         h_sb = held.tile([P, KB, N], BF16, name="h_sb")
         nc.sync.dma_start(h_sb[:], h_prev.rearrange("(k p) n -> p k n", p=P))
         emb_sb = held.tile([P, KB, N], BF16, name="emb_sb")
-        nc.scalar.dma_start(emb_sb[:], emb.rearrange("(k p) n -> p k n", p=P))
-
-        b_blocks = held.tile([P, T], F32, name="b_blocks", align_bytes=64)
-        nc.gpsimd.memset(b_blocks[:], 0.0)
-        b_runs = b.rearrange("(g a c) o -> a g (c o)", a=P // T, c=T)
-        for a in range(P // T):
-            nc.scalar.dma_start(b_blocks[a * T : a * T + Q * CB, :], b_runs[a])
+        nc.sync.dma_start(emb_sb[:], emb.rearrange("(k p) n -> p k n", p=P))
 
         w_sb = {}
         for piece, (first_gate, gates) in enumerate(((GATE_I, 2), (GATE_U, 1), (GATE_O, 1))):
@@ -58,9 +54,6 @@ def tile_capatt_kernel(tc, base, emb, h_prev, c_prev, w_ih, w_hh, b, offs, out):
 
         relu_sb = held.tile([P, KB, N], BF16, name="relu_sb")
         nc.vector.tensor_scalar_max(relu_sb[:], emb_sb[:], 0.0)
-
-        bias_sb = held.tile([P, T], F32, name="bias_sb", align_bytes=64)
-        nc.vector.transpose(bias_sb[:], b_blocks[:])
 
         x_of = {"hh": h_sb, "ih": relu_sb}
         func_of = {GATE_I: SIGMOID, GATE_F: SIGMOID, GATE_U: TANH, GATE_O: SIGMOID}

@@ -5,7 +5,7 @@ C, E, S, N, Q = 256, 256, 512, 128, 4
 CB = C // P
 KB = E // P
 GATE_I, GATE_F, GATE_U, GATE_O = 0, 1, 2, 3
-WARM_MATMULS = 20
+WARM_MATMULS = 26
 
 FLOPS = 2 * (E + C) * Q * C * N
 
@@ -22,7 +22,7 @@ def tile_capatt_kernel(tc, base, emb, h_prev, c_prev, w_ih, w_hh, b, offs, out):
         tc.psum_pool(name="psum_z", bufs=7) as psum_z,
     ):
         warm_sb = held.tile([P, P], BF16, name="warm_sb")
-        nc.vector.memset(warm_sb[:], 0.0)
+        nc.gpsimd.memset(warm_sb[:], 0.0)
         warm_ps = psum_warm.tile([P, P], F32, name="warm_ps")
         for i in range(WARM_MATMULS):
             nc.tensor.matmul(warm_ps[:], warm_sb[:], warm_sb[:], start=True, stop=True)
@@ -31,16 +31,16 @@ def tile_capatt_kernel(tc, base, emb, h_prev, c_prev, w_ih, w_hh, b, offs, out):
         with nc.allow_non_contiguous_dma(reason="b is turned from rows into columns by the load"):
             nc.scalar.dma_start(bias_sb[:], b.rearrange("(g p) o -> p (g o)", p=P))
         h_sb = held.tile([P, KB, N], BF16, name="h_sb")
-        nc.sync.dma_start(h_sb[:], h_prev.rearrange("(k p) n -> p k n", p=P))
+        nc.sync.dma_start(h_sb[:], h_prev.rearrange("(p k) n -> p k n", k=KB))
         emb_sb = held.tile([P, KB, N], BF16, name="emb_sb")
-        nc.sync.dma_start(emb_sb[:], emb.rearrange("(k p) n -> p k n", p=P))
+        nc.sync.dma_start(emb_sb[:], emb.rearrange("(p k) n -> p k n", k=KB))
 
         w_sb = {}
         for piece, (first_gate, gates) in enumerate(((GATE_I, 2), (GATE_U, 1), (GATE_O, 1))):
             for name, w in (("hh", w_hh), ("ih", w_ih)):
                 w_piece = held.tile([P, KB, gates * C], BF16, name=f"w_{name}{piece}")
                 cols = w[:, first_gate * C : (first_gate + gates) * C]
-                nc.sync.dma_start(w_piece[:], cols.rearrange("(k p) r -> p k r", p=P))
+                nc.sync.dma_start(w_piece[:], cols.rearrange("(p k) r -> p k r", k=KB))
                 for q in range(first_gate, first_gate + gates):
                     w_sb[name, q] = w_piece[:, :, (q - first_gate) * C : (q - first_gate + 1) * C]
 

@@ -5,13 +5,16 @@ C, E, S, N, Q = 256, 256, 512, 128, 4
 CB = C // P
 KB = E // P
 GATE_I, GATE_F, GATE_U, GATE_O = 0, 1, 2, 3
-WARM_MATMULS = 26
+WARM_MATMULS = 22
 
 FLOPS = 2 * (E + C) * Q * C * N
 
 BF16, F32, U16 = mybir.dt.bfloat16, mybir.dt.float32, mybir.dt.uint16
 MULT, ADD = mybir.AluOpType.mult, mybir.AluOpType.add
 SIGMOID, TANH = mybir.ActivationFunctionType.Sigmoid, mybir.ActivationFunctionType.Tanh
+
+
+PIECES = ((GATE_I, GATE_F), (GATE_U,), (GATE_O,))
 
 
 def tile_capatt_kernel(tc, base, emb, h_prev, c_prev, w_ih, w_hh, b, offs, out):
@@ -33,19 +36,21 @@ def tile_capatt_kernel(tc, base, emb, h_prev, c_prev, w_ih, w_hh, b, offs, out):
         h_sb = held.tile([P, KB, N], BF16, name="h_sb")
         nc.sync.dma_start(h_sb[:], h_prev.rearrange("(p k) n -> p k n", k=KB))
         emb_sb = held.tile([P, KB, N], BF16, name="emb_sb")
-        nc.sync.dma_start(emb_sb[:], emb.rearrange("(p k) n -> p k n", k=KB))
+        c_sb = held.tile([P, CB, N], F32, name="c_sb")
 
         w_sb = {}
-        for piece, (first_gate, gates) in enumerate(((GATE_I, 2), (GATE_U, 1), (GATE_O, 1))):
+        for piece, gates in enumerate(PIECES):
             for name, w in (("hh", w_hh), ("ih", w_ih)):
-                w_piece = held.tile([P, KB, gates * C], BF16, name=f"w_{name}{piece}")
-                cols = w[:, first_gate * C : (first_gate + gates) * C]
+                w_piece = held.tile([P, KB, len(gates) * C], BF16, name=f"w_{name}{piece}")
+                cols = w[:, gates[0] * C : (gates[-1] + 1) * C]
                 nc.sync.dma_start(w_piece[:], cols.rearrange("(p k) r -> p k r", k=KB))
-                for q in range(first_gate, first_gate + gates):
-                    w_sb[name, q] = w_piece[:, :, (q - first_gate) * C : (q - first_gate + 1) * C]
+                for q in gates:
+                    w_sb[name, q] = w_piece[:, :, (q - gates[0]) * C : (q - gates[0] + 1) * C]
+                if piece == 0 and name == "hh":
+                    nc.sync.dma_start(emb_sb[:], emb.rearrange("(p k) n -> p k n", k=KB))
+            if gates == (GATE_U,):
+                nc.sync.dma_start(c_sb[:], c_prev.rearrange("(k p) n -> p k n", p=P))
 
-        c_sb = held.tile([P, CB, N], F32, name="c_sb")
-        nc.sync.dma_start(c_sb[:], c_prev.rearrange("(k p) n -> p k n", p=P))
         offsets = held.tile([P, N // 16], U16, name="offsets")
         nc.sync.dma_start(offsets[:], offs)
         windows = [held.tile([P, S], F32, name=f"window{cb}") for cb in range(CB)]
@@ -77,32 +82,26 @@ def tile_capatt_kernel(tc, base, emb, h_prev, c_prev, w_ih, w_hh, b, offs, out):
             gate[q, cb] = held.tile([P, N], F32, name=f"gate{q}_{cb}")
             nc.scalar.activation(gate[q, cb][:], z[q, cb][:], func_of[q], bias=bias_sb[:, g : g + 1])
 
-        for cb in range(CB):
-            for q in (GATE_I, GATE_F):
-                add_part(q, cb, "hh")
+        for gates in PIECES:
+            for name in ("hh", "ih"):
+                for cb in range(CB):
+                    for q in gates:
+                        add_part(q, cb, name)
+                        if name == "ih" and q != GATE_O:
+                            activate(q, cb)
 
-        c_new = {}
+        kept = {}
         for cb in range(CB):
-            for q in (GATE_I, GATE_F):
-                add_part(q, cb, "ih")
-                activate(q, cb)
-            add_part(GATE_U, cb, "hh")
-            add_part(GATE_U, cb, "ih")
-            activate(GATE_U, cb)
-            kept = held.tile([P, N], F32, name=f"kept{cb}")
-            nc.vector.tensor_tensor(kept[:], gate[GATE_F, cb][:], c_sb[:, cb, :], MULT)
+            kept[cb] = held.tile([P, N], F32, name=f"kept{cb}")
+            nc.vector.tensor_tensor(kept[cb][:], gate[GATE_F, cb][:], c_sb[:, cb, :], MULT)
+
+        for cb in range(CB):
             fresh = held.tile([P, N], F32, name=f"fresh{cb}")
             nc.vector.tensor_tensor(fresh[:], gate[GATE_I, cb][:], gate[GATE_U, cb][:], MULT)
-            c_new[cb] = held.tile([P, N], F32, name=f"c_new{cb}")
-            nc.vector.tensor_tensor(c_new[cb][:], kept[:], fresh[:], ADD)
-
-        for cb in range(CB):
-            add_part(GATE_O, cb, "hh")
-            add_part(GATE_O, cb, "ih")
-            activate(GATE_O, cb)
-
-        for cb in range(CB):
+            c_new = held.tile([P, N], F32, name=f"c_new{cb}")
+            nc.vector.tensor_tensor(c_new[:], kept[cb][:], fresh[:], ADD)
             tanh_c = held.tile([P, N], F32, name=f"tanh_c{cb}")
-            nc.scalar.activation(tanh_c[:], c_new[cb][:], TANH)
+            nc.scalar.activation(tanh_c[:], c_new[:], TANH)
+            activate(GATE_O, cb)
             nc.vector.tensor_tensor(windows[cb][:].indirect(offsets[:]), gate[GATE_O, cb][:], tanh_c[:], MULT)
             nc.sync.dma_start(out[cb * P : (cb + 1) * P, :], windows[cb][:])

@@ -14,7 +14,7 @@ MULT, ADD = mybir.AluOpType.mult, mybir.AluOpType.add
 SIGMOID, TANH = mybir.ActivationFunctionType.Sigmoid, mybir.ActivationFunctionType.Tanh
 
 
-PIECES = ((GATE_I, GATE_F), (GATE_U,), (GATE_O,))
+PIECES = ((GATE_I, GATE_F, GATE_U), (GATE_O,))
 
 
 def tile_capatt_kernel(tc, base, emb, h_prev, c_prev, w_ih, w_hh, b, offs, out):
@@ -30,9 +30,9 @@ def tile_capatt_kernel(tc, base, emb, h_prev, c_prev, w_ih, w_hh, b, offs, out):
         for i in range(WARM_MATMULS):
             nc.tensor.matmul(warm_ps[:], warm_sb[:], warm_sb[:], start=True, stop=True)
 
-        bias_sb = held.tile([P, Q * CB], F32, name="bias_sb")
+        bias_sb = held.tile([P, Q, CB], F32, name="bias_sb")
         with nc.allow_non_contiguous_dma(reason="b is turned from rows into columns by the load"):
-            nc.scalar.dma_start(bias_sb[:], b.rearrange("(g p) o -> p (g o)", p=P))
+            nc.scalar.dma_start(bias_sb[:], b.rearrange("(q p cb) o -> p q (cb o)", q=Q, cb=CB))
         h_sb = held.tile([P, KB, N], BF16, name="h_sb")
         nc.sync.dma_start(h_sb[:], h_prev.rearrange("(p k) n -> p k n", k=KB))
         emb_sb = held.tile([P, KB, N], BF16, name="emb_sb")
@@ -48,14 +48,16 @@ def tile_capatt_kernel(tc, base, emb, h_prev, c_prev, w_ih, w_hh, b, offs, out):
                     w_sb[name, q] = w_piece[:, :, (q - gates[0]) * C : (q - gates[0] + 1) * C]
                 if piece == 0 and name == "hh":
                     nc.sync.dma_start(emb_sb[:], emb.rearrange("(p k) n -> p k n", k=KB))
-            if gates == (GATE_U,):
-                nc.sync.dma_start(c_sb[:], c_prev.rearrange("(k p) n -> p k n", p=P))
+            if piece == 0:
+                nc.sync.dma_start(c_sb[:], c_prev.rearrange("(p cb) n -> p cb n", cb=CB))
 
         offsets = held.tile([P, N // 16], U16, name="offsets")
         nc.sync.dma_start(offsets[:], offs)
         windows = [held.tile([P, S], F32, name=f"window{cb}") for cb in range(CB)]
+        base_blocks = base.rearrange("(p cb) s -> cb p s", cb=CB)
+        out_blocks = out.rearrange("(p cb) s -> cb p s", cb=CB)
         for cb in range(CB):
-            nc.sync.dma_start(windows[cb][:], base[cb * P : (cb + 1) * P, :])
+            nc.sync.dma_start(windows[cb][:], base_blocks[cb])
 
         relu_sb = held.tile([P, KB, N], BF16, name="relu_sb")
         nc.vector.tensor_scalar_max(relu_sb[:], emb_sb[:], 0.0)
@@ -71,37 +73,38 @@ def tile_capatt_kernel(tc, base, emb, h_prev, c_prev, w_ih, w_hh, b, offs, out):
             for k in range(KB):
                 nc.tensor.matmul(
                     z[q, cb][:],
-                    w_sb[name, q][:, k, cb * P : (cb + 1) * P],
+                    w_sb[name, q][:, k, cb:C:CB],
                     x_of[name][:, k, :],
                     start=(name == "hh" and k == 0),
                     stop=(name == "ih" and k == KB - 1),
                 )
 
         def activate(q, cb):
-            g = q * CB + cb
             gate[q, cb] = held.tile([P, N], F32, name=f"gate{q}_{cb}")
-            nc.scalar.activation(gate[q, cb][:], z[q, cb][:], func_of[q], bias=bias_sb[:, g : g + 1])
-
-        for gates in PIECES:
-            for name in ("hh", "ih"):
-                for cb in range(CB):
-                    for q in gates:
-                        add_part(q, cb, name)
-                        if name == "ih" and q != GATE_O:
-                            activate(q, cb)
-
-        kept = {}
-        for cb in range(CB):
-            kept[cb] = held.tile([P, N], F32, name=f"kept{cb}")
-            nc.vector.tensor_tensor(kept[cb][:], gate[GATE_F, cb][:], c_sb[:, cb, :], MULT)
+            nc.scalar.activation(gate[q, cb][:], z[q, cb][:], func_of[q], bias=bias_sb[:, q, cb : cb + 1])
 
         for cb in range(CB):
+            for q in (GATE_I, GATE_F, GATE_U):
+                add_part(q, cb, "hh")
+
+        c_new = {}
+        for cb in range(CB):
+            for q in (GATE_I, GATE_F, GATE_U):
+                add_part(q, cb, "ih")
+                activate(q, cb)
+            kept = held.tile([P, N], F32, name=f"kept{cb}")
+            nc.vector.tensor_tensor(kept[:], gate[GATE_F, cb][:], c_sb[:, cb, :], MULT)
             fresh = held.tile([P, N], F32, name=f"fresh{cb}")
             nc.vector.tensor_tensor(fresh[:], gate[GATE_I, cb][:], gate[GATE_U, cb][:], MULT)
-            c_new = held.tile([P, N], F32, name=f"c_new{cb}")
-            nc.vector.tensor_tensor(c_new[:], kept[cb][:], fresh[:], ADD)
-            tanh_c = held.tile([P, N], F32, name=f"tanh_c{cb}")
-            nc.scalar.activation(tanh_c[:], c_new[:], TANH)
+            c_new[cb] = held.tile([P, N], F32, name=f"c_new{cb}")
+            nc.vector.tensor_tensor(c_new[cb][:], kept[:], fresh[:], ADD)
+
+        for cb in range(CB):
+            add_part(GATE_O, cb, "hh")
+            add_part(GATE_O, cb, "ih")
+        for cb in range(CB):
             activate(GATE_O, cb)
+            tanh_c = held.tile([P, N], F32, name=f"tanh_c{cb}")
+            nc.scalar.activation(tanh_c[:], c_new[cb][:], TANH)
             nc.vector.tensor_tensor(windows[cb][:].indirect(offsets[:]), gate[GATE_O, cb][:], tanh_c[:], MULT)
-            nc.sync.dma_start(out[cb * P : (cb + 1) * P, :], windows[cb][:])
+            nc.sync.dma_start(out_blocks[cb], windows[cb][:])

@@ -5,6 +5,7 @@ C, E, S, N, Q = 256, 256, 512, 128, 4
 CB = C // P
 KB = E // P
 GATE_I, GATE_F, GATE_U, GATE_O = 0, 1, 2, 3
+BIAS_PITCH = 8
 WARM_MATMULS = 22
 
 FLOPS = 2 * (E + C) * Q * C * N
@@ -30,9 +31,9 @@ def tile_capatt_kernel(tc, base, emb, h_prev, c_prev, w_ih, w_hh, b, offs, out):
         for i in range(WARM_MATMULS):
             nc.tensor.matmul(warm_ps[:], warm_sb[:], warm_sb[:], start=True, stop=True)
 
-        bias_sb = held.tile([P, Q, CB], F32, name="bias_sb")
+        bias_sb = held.tile([P, Q, BIAS_PITCH], F32, name="bias_sb")
         with nc.allow_non_contiguous_dma(reason="b is turned from rows into columns by the load"):
-            nc.scalar.dma_start(bias_sb[:], b.rearrange("(q p cb) o -> p q (cb o)", q=Q, cb=CB))
+            nc.scalar.dma_start(bias_sb[:, :, 0:CB], b.rearrange("(q p cb) o -> p q (cb o)", q=Q, cb=CB))
         h_sb = held.tile([P, KB, N], BF16, name="h_sb")
         nc.sync.dma_start(h_sb[:], h_prev.rearrange("(p k) n -> p k n", k=KB))
         emb_sb = held.tile([P, KB, N], BF16, name="emb_sb")

@@ -33,7 +33,7 @@ def tile_capatt_kernel(tc, base, emb, h_prev, c_prev, w_ih, w_hh, b, offs, out):
 
         bias_sb = held.tile([P, Q, BIAS_PITCH], F32, name="bias_sb")
         with nc.allow_non_contiguous_dma(reason="b is turned from rows into columns by the load"):
-            nc.scalar.dma_start(bias_sb[:, :, 0:CB], b.rearrange("(q p cb) o -> p q (cb o)", q=Q, cb=CB))
+            nc.sync.dma_start(bias_sb[:, :, 0:CB], b.rearrange("(q p cb) o -> p q (cb o)", q=Q, cb=CB))
         h_sb = held.tile([P, KB, N], BF16, name="h_sb")
         nc.sync.dma_start(h_sb[:], h_prev.rearrange("(p k) n -> p k n", k=KB))
         emb_sb = held.tile([P, KB, N], BF16, name="emb_sb")

@@ -6,7 +6,7 @@ CB = C // P
 KB = E // P
 GATE_I, GATE_F, GATE_U, GATE_O = 0, 1, 2, 3
 BIAS_PITCH = 8
-WARM_MATMULS = 22
+WARM_MATMULS = 19
 
 FLOPS = 2 * (E + C) * Q * C * N
 
@@ -32,8 +32,9 @@ def tile_capatt_kernel(tc, base, emb, h_prev, c_prev, w_ih, w_hh, b, offs, out):
             nc.tensor.matmul(warm_ps[:], warm_sb[:], warm_sb[:], start=True, stop=True)
 
         bias_sb = held.tile([P, Q, BIAS_PITCH], F32, name="bias_sb")
+        b_columns = b.rearrange("(q p cb) o -> p q (cb o)", q=Q, cb=CB)
         with nc.allow_non_contiguous_dma(reason="b is turned from rows into columns by the load"):
-            nc.sync.dma_start(bias_sb[:, :, 0:CB], b.rearrange("(q p cb) o -> p q (cb o)", q=Q, cb=CB))
+            nc.sync.dma_start(bias_sb[:, GATE_I : GATE_I + 1, 0:CB], b_columns[:, GATE_I : GATE_I + 1, :])
         h_sb = held.tile([P, KB, N], BF16, name="h_sb")
         nc.sync.dma_start(h_sb[:], h_prev.rearrange("(p k) n -> p k n", k=KB))
         emb_sb = held.tile([P, KB, N], BF16, name="emb_sb")
@@ -50,6 +51,8 @@ def tile_capatt_kernel(tc, base, emb, h_prev, c_prev, w_ih, w_hh, b, offs, out):
                 if piece == 0 and name == "hh":
                     nc.sync.dma_start(emb_sb[:], emb.rearrange("(p k) n -> p k n", k=KB))
             if piece == 0:
+                with nc.allow_non_contiguous_dma(reason="b is turned from rows into columns by the load"):
+                    nc.sync.dma_start(bias_sb[:, GATE_F:Q, 0:CB], b_columns[:, GATE_F:Q, :])
                 nc.sync.dma_start(c_sb[:], c_prev.rearrange("(p cb) n -> p cb n", cb=CB))
 
         offsets = held.tile([P, N // 16], U16, name="offsets")

@@ -5,8 +5,8 @@ C, E, S, N, Q = 256, 256, 512, 128, 4
 CB = C // P
 KB = E // P
 GATE_I, GATE_F, GATE_U, GATE_O = 0, 1, 2, 3
+WARM_MATMULS = 16
 BIAS_PITCH = 8
-WARM_MATMULS = 19
 
 FLOPS = 2 * (E + C) * Q * C * N
 
@@ -15,7 +15,7 @@ MULT, ADD = mybir.AluOpType.mult, mybir.AluOpType.add
 SIGMOID, TANH = mybir.ActivationFunctionType.Sigmoid, mybir.ActivationFunctionType.Tanh
 
 
-PIECES = ((GATE_I, GATE_F, GATE_U), (GATE_O,))
+CELL_GATES = (GATE_I, GATE_F, GATE_U)
 
 
 def tile_capatt_kernel(tc, base, emb, h_prev, c_prev, w_ih, w_hh, b, offs, out):
@@ -35,26 +35,33 @@ def tile_capatt_kernel(tc, base, emb, h_prev, c_prev, w_ih, w_hh, b, offs, out):
         b_columns = b.rearrange("(q p cb) o -> p q (cb o)", q=Q, cb=CB)
         with nc.allow_non_contiguous_dma(reason="b is turned from rows into columns by the load"):
             nc.sync.dma_start(bias_sb[:, GATE_I : GATE_I + 1, 0:CB], b_columns[:, GATE_I : GATE_I + 1, :])
+
+        w_gate = {}
         h_sb = held.tile([P, KB, N], BF16, name="h_sb")
         nc.sync.dma_start(h_sb[:], h_prev.rearrange("(p k) n -> p k n", k=KB))
+        for k in range(KB):
+            w_piece = held.tile([P, len(CELL_GATES) * C], BF16, name=f"w_hh_cell{k}")
+            nc.sync.dma_start(w_piece[:], w_hh.rearrange("(p k) r -> k p r", k=KB)[k][:, 0 : len(CELL_GATES) * C])
+            for q in CELL_GATES:
+                w_gate["hh", q, k] = w_piece[:, q * C : (q + 1) * C]
         emb_sb = held.tile([P, KB, N], BF16, name="emb_sb")
+        nc.sync.dma_start(emb_sb[:], emb.rearrange("(p k) n -> p k n", k=KB))
+
+        def load_gates(name, w, gates):
+            w_piece = held.tile([P, KB, len(gates) * C], BF16, name=f"w_{name}{gates[0]}")
+            cols = w[:, gates[0] * C : (gates[-1] + 1) * C]
+            nc.sync.dma_start(w_piece[:], cols.rearrange("(p k) r -> p k r", k=KB))
+            for q in gates:
+                for k in range(KB):
+                    w_gate[name, q, k] = w_piece[:, k, (q - gates[0]) * C : (q - gates[0] + 1) * C]
+
+        load_gates("ih", w_ih, CELL_GATES)
+        with nc.allow_non_contiguous_dma(reason="b is turned from rows into columns by the load"):
+            nc.sync.dma_start(bias_sb[:, GATE_F:Q, 0:CB], b_columns[:, GATE_F:Q, :])
         c_sb = held.tile([P, CB, N], F32, name="c_sb")
-
-        w_sb = {}
-        for piece, gates in enumerate(PIECES):
-            for name, w in (("hh", w_hh), ("ih", w_ih)):
-                w_piece = held.tile([P, KB, len(gates) * C], BF16, name=f"w_{name}{piece}")
-                cols = w[:, gates[0] * C : (gates[-1] + 1) * C]
-                nc.sync.dma_start(w_piece[:], cols.rearrange("(p k) r -> p k r", k=KB))
-                for q in gates:
-                    w_sb[name, q] = w_piece[:, :, (q - gates[0]) * C : (q - gates[0] + 1) * C]
-                if piece == 0 and name == "hh":
-                    nc.sync.dma_start(emb_sb[:], emb.rearrange("(p k) n -> p k n", k=KB))
-            if piece == 0:
-                with nc.allow_non_contiguous_dma(reason="b is turned from rows into columns by the load"):
-                    nc.sync.dma_start(bias_sb[:, GATE_F:Q, 0:CB], b_columns[:, GATE_F:Q, :])
-                nc.sync.dma_start(c_sb[:], c_prev.rearrange("(p cb) n -> p cb n", cb=CB))
-
+        nc.sync.dma_start(c_sb[:], c_prev.rearrange("(p cb) n -> p cb n", cb=CB))
+        load_gates("hh", w_hh, (GATE_O,))
+        load_gates("ih", w_ih, (GATE_O,))
         offsets = held.tile([P, N // 16], U16, name="offsets")
         nc.sync.dma_start(offsets[:], offs)
         windows = [held.tile([P, S], F32, name=f"window{cb}") for cb in range(CB)]
@@ -65,36 +72,37 @@ def tile_capatt_kernel(tc, base, emb, h_prev, c_prev, w_ih, w_hh, b, offs, out):
 
         relu_sb = held.tile([P, KB, N], BF16, name="relu_sb")
         nc.vector.tensor_scalar_max(relu_sb[:], emb_sb[:], 0.0)
+        moving = {"hh": h_sb, "ih": relu_sb}
 
-        x_of = {"hh": h_sb, "ih": relu_sb}
         func_of = {GATE_I: SIGMOID, GATE_F: SIGMOID, GATE_U: TANH, GATE_O: SIGMOID}
         z = {}
         gate = {}
 
-        def add_part(q, cb, name):
-            if name == "hh":
+        def add_part(q, cb, name, k):
+            if (name, k) == ("hh", 0):
                 z[q, cb] = psum_z.tile([P, N], F32, name="z")
-            for k in range(KB):
-                nc.tensor.matmul(
-                    z[q, cb][:],
-                    w_sb[name, q][:, k, cb:C:CB],
-                    x_of[name][:, k, :],
-                    start=(name == "hh" and k == 0),
-                    stop=(name == "ih" and k == KB - 1),
-                )
+            nc.tensor.matmul(
+                z[q, cb][:],
+                w_gate[name, q, k][:, cb:C:CB],
+                moving[name][:, k, :],
+                start=((name, k) == ("hh", 0)),
+                stop=((name, k) == ("ih", KB - 1)),
+            )
 
         def activate(q, cb):
             gate[q, cb] = held.tile([P, N], F32, name=f"gate{q}_{cb}")
             nc.scalar.activation(gate[q, cb][:], z[q, cb][:], func_of[q], bias=bias_sb[:, q, cb : cb + 1])
 
-        for cb in range(CB):
-            for q in (GATE_I, GATE_F, GATE_U):
-                add_part(q, cb, "hh")
+        for k in range(KB):
+            for cb in range(CB):
+                for q in CELL_GATES:
+                    add_part(q, cb, "hh", k)
 
         c_new = {}
         for cb in range(CB):
-            for q in (GATE_I, GATE_F, GATE_U):
-                add_part(q, cb, "ih")
+            for q in CELL_GATES:
+                for k in range(KB):
+                    add_part(q, cb, "ih", k)
                 activate(q, cb)
             kept = held.tile([P, N], F32, name=f"kept{cb}")
             nc.vector.tensor_tensor(kept[:], gate[GATE_F, cb][:], c_sb[:, cb, :], MULT)
@@ -104,8 +112,9 @@ def tile_capatt_kernel(tc, base, emb, h_prev, c_prev, w_ih, w_hh, b, offs, out):
             nc.vector.tensor_tensor(c_new[cb][:], kept[:], fresh[:], ADD)
 
         for cb in range(CB):
-            add_part(GATE_O, cb, "hh")
-            add_part(GATE_O, cb, "ih")
+            for name in ("hh", "ih"):
+                for k in range(KB):
+                    add_part(GATE_O, cb, name, k)
         for cb in range(CB):
             activate(GATE_O, cb)
             tanh_c = held.tile([P, N], F32, name=f"tanh_c{cb}")

@@ -37,15 +37,20 @@ def tile_capatt_kernel(tc, base, emb, h_prev, c_prev, w_ih, w_hh, b, offs, out):
             nc.sync.dma_start(bias_sb[:, GATE_I : GATE_I + 1, 0:CB], b_columns[:, GATE_I : GATE_I + 1, :])
 
         w_gate = {}
+
+        def load_cell_gates(name, w):
+            for k in range(KB):
+                w_piece = held.tile([P, len(CELL_GATES) * C], BF16, name=f"w_{name}_cell{k}")
+                nc.sync.dma_start(w_piece[:], w.rearrange("(p k) r -> k p r", k=KB)[k][:, 0 : len(CELL_GATES) * C])
+                for q in CELL_GATES:
+                    w_gate[name, q, k] = w_piece[:, q * C : (q + 1) * C]
+
         h_sb = held.tile([P, KB, N], BF16, name="h_sb")
         nc.sync.dma_start(h_sb[:], h_prev.rearrange("(p k) n -> p k n", k=KB))
-        for k in range(KB):
-            w_piece = held.tile([P, len(CELL_GATES) * C], BF16, name=f"w_hh_cell{k}")
-            nc.sync.dma_start(w_piece[:], w_hh.rearrange("(p k) r -> k p r", k=KB)[k][:, 0 : len(CELL_GATES) * C])
-            for q in CELL_GATES:
-                w_gate["hh", q, k] = w_piece[:, q * C : (q + 1) * C]
+        load_cell_gates("hh", w_hh)
         emb_sb = held.tile([P, KB, N], BF16, name="emb_sb")
         nc.sync.dma_start(emb_sb[:], emb.rearrange("(p k) n -> p k n", k=KB))
+        load_cell_gates("ih", w_ih)
 
         def load_gates(name, w, gates):
             w_piece = held.tile([P, KB, len(gates) * C], BF16, name=f"w_{name}{gates[0]}")
@@ -55,7 +60,6 @@ def tile_capatt_kernel(tc, base, emb, h_prev, c_prev, w_ih, w_hh, b, offs, out):
                 for k in range(KB):
                     w_gate[name, q, k] = w_piece[:, k, (q - gates[0]) * C : (q - gates[0] + 1) * C]
 
-        load_gates("ih", w_ih, CELL_GATES)
         with nc.allow_non_contiguous_dma(reason="b is turned from rows into columns by the load"):
             nc.sync.dma_start(bias_sb[:, GATE_F:Q, 0:CB], b_columns[:, GATE_F:Q, :])
         c_sb = held.tile([P, CB, N], F32, name="c_sb")
@@ -100,9 +104,10 @@ def tile_capatt_kernel(tc, base, emb, h_prev, c_prev, w_ih, w_hh, b, offs, out):
 
         c_new = {}
         for cb in range(CB):
-            for q in CELL_GATES:
-                for k in range(KB):
+            for k in range(KB):
+                for q in CELL_GATES:
                     add_part(q, cb, "ih", k)
+            for q in CELL_GATES:
                 activate(q, cb)
             kept = held.tile([P, N], F32, name=f"kept{cb}")
             nc.vector.tensor_tensor(kept[:], gate[GATE_F, cb][:], c_sb[:, cb, :], MULT)

@@ -31,6 +31,8 @@ def tile_capatt_kernel(tc, base, emb, h_prev, c_prev, w_ih, w_hh, b, offs, out):
         for i in range(WARM_MATMULS):
             nc.tensor.matmul(warm_ps[:], warm_sb[:], warm_sb[:], start=True, stop=True)
 
+        h_sb = held.tile([P, KB, N], BF16, name="h_sb")
+        nc.sync.dma_start(h_sb[:], h_prev.rearrange("(p k) n -> p k n", k=KB))
         bias_sb = held.tile([P, Q, BIAS_PITCH], F32, name="bias_sb")
         b_columns = b.rearrange("(q p cb) o -> p q (cb o)", q=Q, cb=CB)
         with nc.allow_non_contiguous_dma(reason="b is turned from rows into columns by the load"):
@@ -45,8 +47,6 @@ def tile_capatt_kernel(tc, base, emb, h_prev, c_prev, w_ih, w_hh, b, offs, out):
                 for q in CELL_GATES:
                     w_gate[name, q, k] = w_piece[:, q * C : (q + 1) * C]
 
-        h_sb = held.tile([P, KB, N], BF16, name="h_sb")
-        nc.sync.dma_start(h_sb[:], h_prev.rearrange("(p k) n -> p k n", k=KB))
         load_cell_gates("hh", w_hh)
         emb_sb = held.tile([P, KB, N], BF16, name="emb_sb")
         nc.sync.dma_start(emb_sb[:], emb.rearrange("(p k) n -> p k n", k=KB))

import concourse.mybir as mybir

P = 128
C, E, S, N, Q = 256, 256, 512, 128, 4
CB = C // P
KB = E // P
GATE_I, GATE_F, GATE_U, GATE_O = 0, 1, 2, 3
WARM_MATMULS = 16
BIAS_PITCH = 8

FLOPS = 2 * (E + C) * Q * C * N

BF16, F32, U16 = mybir.dt.bfloat16, mybir.dt.float32, mybir.dt.uint16
MULT, ADD = mybir.AluOpType.mult, mybir.AluOpType.add
SIGMOID, TANH = mybir.ActivationFunctionType.Sigmoid, mybir.ActivationFunctionType.Tanh


CELL_GATES = (GATE_I, GATE_F, GATE_U)


def tile_capatt_kernel(tc, base, emb, h_prev, c_prev, w_ih, w_hh, b, offs, out):
    nc = tc.nc
    with (
        tc.tile_pool(name="held", bufs=1) as held,
        tc.psum_pool(name="psum_warm", bufs=1) as psum_warm,
        tc.psum_pool(name="psum_z", bufs=7) as psum_z,
    ):
        warm_sb = held.tile([P, P], BF16, name="warm_sb")
        nc.gpsimd.memset(warm_sb[:], 0.0)
        warm_ps = psum_warm.tile([P, P], F32, name="warm_ps")
        for i in range(WARM_MATMULS):
            nc.tensor.matmul(warm_ps[:], warm_sb[:], warm_sb[:], start=True, stop=True)

        h_sb = held.tile([P, KB, N], BF16, name="h_sb")
        nc.sync.dma_start(h_sb[:], h_prev.rearrange("(p k) n -> p k n", k=KB))
        bias_sb = held.tile([P, Q, BIAS_PITCH], F32, name="bias_sb")
        b_columns = b.rearrange("(q p cb) o -> p q (cb o)", q=Q, cb=CB)
        with nc.allow_non_contiguous_dma(reason="b is turned from rows into columns by the load"):
            nc.sync.dma_start(bias_sb[:, GATE_I : GATE_I + 1, 0:CB], b_columns[:, GATE_I : GATE_I + 1, :])

        w_gate = {}

        def load_cell_gates(name, w):
            for k in range(KB):
                w_piece = held.tile([P, len(CELL_GATES) * C], BF16, name=f"w_{name}_cell{k}")
                nc.sync.dma_start(w_piece[:], w.rearrange("(p k) r -> k p r", k=KB)[k][:, 0 : len(CELL_GATES) * C])
                for q in CELL_GATES:
                    w_gate[name, q, k] = w_piece[:, q * C : (q + 1) * C]

        load_cell_gates("hh", w_hh)
        emb_sb = held.tile([P, KB, N], BF16, name="emb_sb")
        nc.sync.dma_start(emb_sb[:], emb.rearrange("(p k) n -> p k n", k=KB))
        load_cell_gates("ih", w_ih)

        def load_gates(name, w, gates):
            w_piece = held.tile([P, KB, len(gates) * C], BF16, name=f"w_{name}{gates[0]}")
            cols = w[:, gates[0] * C : (gates[-1] + 1) * C]
            nc.sync.dma_start(w_piece[:], cols.rearrange("(p k) r -> p k r", k=KB))
            for q in gates:
                for k in range(KB):
                    w_gate[name, q, k] = w_piece[:, k, (q - gates[0]) * C : (q - gates[0] + 1) * C]

        with nc.allow_non_contiguous_dma(reason="b is turned from rows into columns by the load"):
            nc.sync.dma_start(bias_sb[:, GATE_F:Q, 0:CB], b_columns[:, GATE_F:Q, :])
        c_sb = held.tile([P, CB, N], F32, name="c_sb")
        nc.sync.dma_start(c_sb[:], c_prev.rearrange("(p cb) n -> p cb n", cb=CB))
        load_gates("hh", w_hh, (GATE_O,))
        load_gates("ih", w_ih, (GATE_O,))
        offsets = held.tile([P, N // 16], U16, name="offsets")
        nc.sync.dma_start(offsets[:], offs)
        windows = [held.tile([P, S], F32, name=f"window{cb}") for cb in range(CB)]
        base_blocks = base.rearrange("(p cb) s -> cb p s", cb=CB)
        out_blocks = out.rearrange("(p cb) s -> cb p s", cb=CB)
        for cb in range(CB):
            nc.sync.dma_start(windows[cb][:], base_blocks[cb])

        relu_sb = held.tile([P, KB, N], BF16, name="relu_sb")
        nc.vector.tensor_scalar_max(relu_sb[:], emb_sb[:], 0.0)
        moving = {"hh": h_sb, "ih": relu_sb}

        func_of = {GATE_I: SIGMOID, GATE_F: SIGMOID, GATE_U: TANH, GATE_O: SIGMOID}
        z = {}
        gate = {}

        def add_part(q, cb, name, k):
            if (name, k) == ("hh", 0):
                z[q, cb] = psum_z.tile([P, N], F32, name="z")
            nc.tensor.matmul(
                z[q, cb][:],
                w_gate[name, q, k][:, cb:C:CB],
                moving[name][:, k, :],
                start=((name, k) == ("hh", 0)),
                stop=((name, k) == ("ih", KB - 1)),
            )

        def activate(q, cb):
            gate[q, cb] = held.tile([P, N], F32, name=f"gate{q}_{cb}")
            nc.scalar.activation(gate[q, cb][:], z[q, cb][:], func_of[q], bias=bias_sb[:, q, cb : cb + 1])

        for k in range(KB):
            for cb in range(CB):
                for q in CELL_GATES:
                    add_part(q, cb, "hh", k)

        c_new = {}
        for cb in range(CB):
            for k in range(KB):
                for q in CELL_GATES:
                    add_part(q, cb, "ih", k)
            for q in CELL_GATES:
                activate(q, cb)
            kept = held.tile([P, N], F32, name=f"kept{cb}")
            nc.vector.tensor_tensor(kept[:], gate[GATE_F, cb][:], c_sb[:, cb, :], MULT)
            fresh = held.tile([P, N], F32, name=f"fresh{cb}")
            nc.vector.tensor_tensor(fresh[:], gate[GATE_I, cb][:], gate[GATE_U, cb][:], MULT)
            c_new[cb] = held.tile([P, N], F32, name=f"c_new{cb}")
            nc.vector.tensor_tensor(c_new[cb][:], kept[:], fresh[:], ADD)

        for cb in range(CB):
            for name in ("hh", "ih"):
                for k in range(KB):
                    add_part(GATE_O, cb, name, k)
        for cb in range(CB):
            activate(GATE_O, cb)
            tanh_c = held.tile([P, N], F32, name=f"tanh_c{cb}")
            nc.scalar.activation(tanh_c[:], c_new[cb][:], TANH)
            nc.vector.tensor_tensor(windows[cb][:].indirect(offsets[:]), gate[GATE_O, cb][:], tanh_c[:], MULT)
            nc.sync.dma_start(out_blocks[cb], windows[cb][:])
